import numpy as np
import ml_dtypes


def mxq(x, axis, fmt="e4m3"):
    dtype, down = {"e4m3": (ml_dtypes.float8_e4m3fn, 7), "e5m2": (ml_dtypes.float8_e5m2, 14)}[fmt]
    v = np.moveaxis(np.asarray(x, np.float32).astype(ml_dtypes.bfloat16).astype(np.float64), axis, -1)
    blocks = v.reshape(v.shape[:-1] + (-1, 32))
    amax = np.abs(blocks).max(-1, keepdims=True)
    byte = np.maximum(np.where(amax > 0, np.frexp(amax)[1] - 1 + 127, 0) - down, 1)
    scale = np.exp2(byte - 127.0)
    codes = (blocks / scale).astype(np.float32).astype(dtype).astype(np.float64)
    return np.moveaxis((codes * scale).reshape(v.shape), -1, axis)


WIDE = False


def mx_kscale(k):
    if not WIDE:
        return np.ones(k)
    levels = np.array([10, -10, 5, -5, 0])
    a = np.random.permutation(np.resize(levels, k // 512 * 4)).reshape(k // 512, 4)
    idx = np.arange(k)
    return np.exp2(a[idx // 512, idx % 128 // 32])


BF16 = ml_dtypes.bfloat16


def bf(x):
    return np.asarray(x, np.float32).astype(BF16)


def f64(x):
    return np.asarray(x).astype(np.float64)


B, DIN, DOUT, ORDER = 16384, 512, 128, 8


def householder_cols(v):
    vn = v / np.sqrt(np.sum(v * v))
    return np.eye(DIN)[:, :DOUT] - 2.0 * vn[:, None] * vn[None, :DOUT]


def setup_inputs():
    s = mx_kscale(DIN)
    return {"x": bf(np.random.standard_normal((B, DIN)) * s),
            "u_prev": bf(np.random.standard_normal((DIN, DIN)) / np.sqrt(DIN) / s[:, None]),
            "v_last": bf(np.random.standard_normal(DIN)),
            "d": bf(np.random.standard_normal(DOUT)),
            "bias": bf(np.random.standard_normal(DOUT) * 0.3)}


def reference(x, u_prev, v_last, d, bias):
    h = householder_cols(f64(v_last))
    u = mxq(f64(u_prev), 1, "e4m3") @ mxq(h, 0, "e4m3")
    w = u * f64(d)[None, :]
    return (mxq(f64(x), 1, "e4m3") @ mxq(w, 0, "e4m3")) + f64(bias)[None, :]

@@ -1,0 +1,219 @@
+from contextlib import ExitStack
+
+import concourse.mybir as mybir
+from concourse.masks import make_identity
+
+BF16 = mybir.dt.bfloat16
+F32 = mybir.dt.float32
+U32 = mybir.dt.uint32
+U8 = mybir.dt.uint8
+FP8X4 = mybir.dt.float8_e4m3fn_x4
+ADD = mybir.AluOpType.add
+MULT = mybir.AluOpType.mult
+SQUARE = mybir.ActivationFunctionType.Square
+
+P = 128
+PACK = 4
+B, DIN, DOUT = 16384, 512, 128
+WORDS = DIN // 2
+
+TILES = 8
+ROUND_ROWS = P * TILES
+ROUNDS = B // ROUND_ROWS
+XT_TILES = 2
+Y_TILES = 4
+LOADS_AHEAD = 12
+
+FLOPS = 2 * B * DIN * DOUT + 2 * DIN * DIN * DOUT
+
+
+def tile_orthogonaldense_pb_t_kernel(tc, x, u_prev, v_last, d, bias, out):
+    nc = tc.nc
+    with ExitStack() as ctx:
+        consts = ctx.enter_context(tc.tile_pool(name="consts", bufs=1))
+        x_pool = ctx.enter_context(tc.tile_pool(name="x_pool", bufs=LOADS_AHEAD))
+        y_pool = ctx.enter_context(tc.tile_pool(name="y_pool", bufs=ROUNDS))
+        work = ctx.enter_context(tc.tile_pool(name="work", bufs=3))
+        psum_t = ctx.enter_context(tc.psum_pool(name="psum_t", bufs=6))
+        psum_y = ctx.enter_context(tc.psum_pool(name="psum_y", bufs=2))
+        ctx.enter_context(tc.manual_schedule())
+
+        x_tiles = {}
+        grouped_tiles = {}
+        code_tiles = {}
+
+        def load_x(i):
+            x_sb = x_pool.tile([P, TILES * DIN], BF16, tag="x_sb")
+            rows = x[i * ROUND_ROWS : (i + 1) * ROUND_ROWS, :]
+            nc.sync.dma_start(out=x_sb[:], in_=rows.rearrange("(p r) k -> p (r k)", r=TILES))
+            x_tiles[i] = x_sb
+
+        def transpose_round(i):
+            x_words = x_tiles[i][:].bitcast(F32)
+            grouped = work.tile([P, TILES * P * PACK], BF16, tag="grouped", align_bytes=64)
+            grouped_words = grouped[:].bitcast(F32).rearrange("p (r m u) -> p r m u", r=TILES, u=2)
+            for r0 in range(0, TILES, XT_TILES):
+                xt = psum_t.tile([P, XT_TILES, 2, P], F32, tag="t")
+                for a in range(XT_TILES):
+                    for u in range(2):
+                        first = (r0 + a) * WORDS + u * P
+                        nc.tensor.transpose(xt[:, a, u, :], x_words[:, first : first + P], ident_f32[:])
+                nc.scalar.copy(
+                    out=grouped_words[:, r0 : r0 + XT_TILES, :, :],
+                    in_=xt[:].rearrange("p a u m -> p a m u"),
+                )
+            grouped_tiles[i] = grouped
+
+        def quantise_round(i):
+            codes = work.tile([P, TILES * P], U32, tag="codes", align_bytes=64)
+            scales = work.tile([P, TILES * P], U8, tag="scales", align_bytes=64)
+            nc.vector.quantize_mx(out=codes[:].bitcast(FP8X4), scales=scales[:], in_=grouped_tiles[i][:])
+            code_tiles[i] = (codes, scales)
+
+        def multiply_round(i):
+            codes, scales = code_tiles[i]
+            y_sb = y_pool.tile([P, TILES, DOUT], F32, tag="y_sb")
+            for r0 in range(0, TILES, Y_TILES):
+                y_ps = psum_y.tile([P, Y_TILES, DOUT], F32, tag="y")
+                for a in range(Y_TILES):
+                    cols = slice((r0 + a) * P, (r0 + a + 1) * P)
+                    nc.tensor.matmul_mx(
+                        out=y_ps[:, a, :],
+                        lhsT=codes[:, cols].bitcast(FP8X4),
+                        lhsT_scale=scales[:, cols],
+                        rhs=w_codes[:].bitcast(FP8X4),
+                        rhs_scale=w_scales[:],
+                        start=True,
+                        stop=True,
+                    )
+                nc.vector.tensor_tensor(
+                    out=y_sb[:, r0 : r0 + Y_TILES, :],
+                    in0=y_ps[:],
+                    in1=bias_all.unsqueeze(1).to_broadcast([P, Y_TILES, DOUT]),
+                    op=ADD,
+                )
+            rows = out[i * ROUND_ROWS : (i + 1) * ROUND_ROWS, :]
+            nc.sync.dma_start(
+                out=rows.rearrange("(p r) j -> p (r j)", r=TILES),
+                in_=y_sb[:].rearrange("p r j -> p (r j)"),
+            )
+
+        ident_bf16 = consts.tile([P, P], BF16)
+        make_identity(nc, ident_bf16[:])
+        ident_f32 = consts.tile([P, P], F32)
+        make_identity(nc, ident_f32[:])
+        ones = consts.tile([P, P], BF16)
+        nc.vector.memset(ones[:], 1.0)
+        vectors = consts.tile([P, DIN + 2 * DOUT], BF16)
+        nc.vector.memset(vectors[:], 0.0)
+        nc.scalar.dma_start(out=vectors[0:1, 0:DIN], in_=v_last.rearrange("(o n) -> o n", o=1))
+        nc.scalar.dma_start(out=vectors[0:1, DIN : DIN + DOUT], in_=d.rearrange("(o n) -> o n", o=1))
+        nc.scalar.dma_start(out=vectors[0:1, DIN + DOUT :], in_=bias.rearrange("(o n) -> o n", o=1))
+        u_sb = consts.tile([P, PACK, DIN], BF16)
+        nc.sync.dma_start(
+            out=u_sb[:].rearrange("p (u e) k -> p u (e k)", u=2),
+            in_=u_prev.rearrange("(u p e) k -> p u (e k)", u=2, e=2),
+        )
+        for i in range(LOADS_AHEAD):
+            load_x(i)
+
+        v_all_ps = psum_t.tile([P, DIN], F32, tag="t")
+        nc.tensor.matmul(v_all_ps[:], lhsT=ones[:], rhs=vectors[:, 0:DIN], start=True, stop=True)
+        d_bias_ps = psum_y.tile([P, 2 * DOUT], F32, tag="y")
+        nc.tensor.matmul(d_bias_ps[:], lhsT=ones[:], rhs=vectors[:, DIN:], start=True, stop=True)
+        vv_ps = psum_t.tile([P, PACK, DOUT], F32, tag="t")
+        for s in range(PACK):
+            nc.tensor.matmul(
+                vv_ps[:, s, :],
+                lhsT=vectors[:, s * P : (s + 1) * P],
+                rhs=vectors[:, 0:DOUT],
+                start=True,
+                stop=True,
+            )
+        v_squares = consts.tile([P, DIN], F32)
+        sum_squares = consts.tile([P, 1], F32)
+        nc.scalar.activation(out=v_squares[:], in_=v_all_ps[:], func=SQUARE, accum_out=sum_squares[:])
+        d_bias = consts.tile([P, 2 * DOUT], F32)
+        nc.scalar.copy(out=d_bias[:], in_=d_bias_ps[:])
+        d_all = d_bias[:, 0:DOUT]
+        bias_all = d_bias[:, DOUT:]
+        minus_half_sum = consts.tile([P, 1], F32)
+        nc.vector.tensor_scalar_mul(out=minus_half_sum[:], in0=sum_squares[:], scalar1=-0.5)
+        minus_two_over_sum = consts.tile([P, 1], F32)
+        nc.vector.reciprocal(out=minus_two_over_sum[:], in_=minus_half_sum[:])
+        h_grouped = consts.tile([P, DOUT, PACK], BF16, align_bytes=64)
+        nc.vector.scalar_tensor_tensor(
+            out=h_grouped[:, :, 0],
+            in0=vv_ps[:, 0, :],
+            scalar=minus_two_over_sum[:, 0:1],
+            in1=ident_f32[:],
+            op0=MULT,
+            op1=ADD,
+        )
+        nc.vector.tensor_scalar_mul(
+            out=h_grouped[:, :, 1:PACK],
+            in0=vv_ps[:, 1:PACK, :].rearrange("p s j -> p j s"),
+            scalar1=minus_two_over_sum[:, 0:1],
+        )
+
+        u_grouped = consts.tile([P, PACK, P, PACK], BF16, align_bytes=64)
+        for t0 in range(0, PACK, 2):
+            ut = psum_t.tile([P, 2, PACK, P], BF16, tag="t")
+            for a in range(2):
+                for s in range(PACK):
+                    nc.tensor.transpose(ut[:, a, s, :], u_sb[:, t0 + a, s * P : (s + 1) * P], ident_bf16[:])
+            copy_out = nc.vector.tensor_copy if t0 == 0 else nc.scalar.copy
+            copy_out(out=u_grouped[:, t0 : t0 + 2, :, :], in_=ut[:].rearrange("p a s m -> p a m s"))
+
+        h_codes = consts.tile([P, DOUT], U32, align_bytes=64)
+        h_scales = consts.tile([P, DOUT], U8, align_bytes=64)
+        nc.vector.quantize_mx(
+            out=h_codes[:].bitcast(FP8X4),
+            scales=h_scales[:],
+            in_=h_grouped[:].rearrange("p j s -> p (j s)"),
+        )
+        u_codes = consts.tile([P, PACK * P], U32, align_bytes=64)
+        u_scales = consts.tile([P, PACK * P], U8, align_bytes=64)
+        nc.vector.quantize_mx(
+            out=u_codes[:].bitcast(FP8X4),
+            scales=u_scales[:],
+            in_=u_grouped[:].rearrange("p t m s -> p (t m s)"),
+        )
+
+        transpose_round(0)
+
+        w_ps = psum_y.tile([P, PACK, DOUT], F32, tag="y")
+        for t in range(PACK):
+            nc.tensor.matmul_mx(
+                out=w_ps[:, t, :],
+                lhsT=u_codes[:, t * P : (t + 1) * P].bitcast(FP8X4),
+                lhsT_scale=u_scales[:, t * P : (t + 1) * P],
+                rhs=h_codes[:].bitcast(FP8X4),
+                rhs_scale=h_scales[:],
+                start=True,
+                stop=True,
+            )
+        w_grouped = consts.tile([P, DOUT, PACK], BF16, align_bytes=64)
+        nc.vector.tensor_tensor(
+            out=w_grouped[:],
+            in0=w_ps[:].rearrange("p t j -> p j t"),
+            in1=d_all.unsqueeze(2).to_broadcast([P, DOUT, PACK]),
+            op=MULT,
+        )
+        w_codes = consts.tile([P, DOUT], U32, align_bytes=64)
+        w_scales = consts.tile([P, DOUT], U8, align_bytes=64)
+        nc.vector.quantize_mx(
+            out=w_codes[:].bitcast(FP8X4),
+            scales=w_scales[:],
+            in_=w_grouped[:].rearrange("p j t -> p (j t)"),
+        )
+
+        for i in range(ROUNDS + 1):
+            if i + LOADS_AHEAD < ROUNDS:
+                load_x(i + LOADS_AHEAD)
+            if i + 1 < ROUNDS:
+                transpose_round(i + 1)
+            if i < ROUNDS:
+                quantise_round(i)
+            if i >= 1:
+                multiply_round(i - 1)

@@ -22,7 +22,7 @@ ROUND_ROWS = P * TILES
 ROUNDS = B // ROUND_ROWS
 XT_TILES = 2
 Y_TILES = 4
-LOADS_AHEAD = 12
+LOADS_AHEAD = 13
 
 FLOPS = 2 * B * DIN * DOUT + 2 * DIN * DIN * DOUT
 
@@ -102,18 +102,18 @@ def tile_orthogonaldense_pb_t_kernel(tc, x, u_prev, v_last, d, bias, out):
         make_identity(nc, ident_bf16[:])
         ident_f32 = consts.tile([P, P], F32)
         make_identity(nc, ident_f32[:])
-        ones = consts.tile([P, P], BF16)
-        nc.vector.memset(ones[:], 1.0)
         vectors = consts.tile([P, DIN + 2 * DOUT], BF16)
         nc.vector.memset(vectors[:], 0.0)
-        nc.scalar.dma_start(out=vectors[0:1, 0:DIN], in_=v_last.rearrange("(o n) -> o n", o=1))
-        nc.scalar.dma_start(out=vectors[0:1, DIN : DIN + DOUT], in_=d.rearrange("(o n) -> o n", o=1))
-        nc.scalar.dma_start(out=vectors[0:1, DIN + DOUT :], in_=bias.rearrange("(o n) -> o n", o=1))
+        ones = consts.tile([P, P], BF16)
+        nc.vector.memset(ones[:], 1.0)
         u_sb = consts.tile([P, PACK, DIN], BF16)
         nc.sync.dma_start(
             out=u_sb[:].rearrange("p (u e) k -> p u (e k)", u=2),
             in_=u_prev.rearrange("(u p e) k -> p u (e k)", u=2, e=2),
         )
+        nc.sync.dma_start(out=vectors[0:1, 0:DIN], in_=v_last.rearrange("(o n) -> o n", o=1))
+        nc.sync.dma_start(out=vectors[0:1, DIN : DIN + DOUT], in_=d.rearrange("(o n) -> o n", o=1))
+        nc.sync.dma_start(out=vectors[0:1, DIN + DOUT :], in_=bias.rearrange("(o n) -> o n", o=1))
         for i in range(LOADS_AHEAD):
             load_x(i)
 
@@ -181,6 +181,7 @@ def tile_orthogonaldense_pb_t_kernel(tc, x, u_prev, v_last, d, bias, out):
         )
 
         transpose_round(0)
+        load_x(LOADS_AHEAD)
 
         w_ps = psum_y.tile([P, PACK, DOUT], F32, tag="y")
         for t in range(PACK):
@@ -209,10 +210,10 @@ def tile_orthogonaldense_pb_t_kernel(tc, x, u_prev, v_last, d, bias, out):
         )
 
         for i in range(ROUNDS + 1):
-            if i + LOADS_AHEAD < ROUNDS:
-                load_x(i + LOADS_AHEAD)
             if i + 1 < ROUNDS:
                 transpose_round(i + 1)
+            if i + 1 + LOADS_AHEAD < ROUNDS:
+                load_x(i + 1 + LOADS_AHEAD)
             if i < ROUNDS:
                 quantise_round(i)
             if i >= 1:

@@ -18,11 +18,16 @@ B, DIN, DOUT = 16384, 512, 128
 WORDS = DIN // 2
 
 TILES = 8
-ROUND_ROWS = P * TILES
-ROUNDS = B // ROUND_ROWS
+ROUNDS = B // (P * TILES)
+CHUNK_TILES = 32
+CHUNK_ROWS = P * CHUNK_TILES
+CHUNK_ROUNDS = CHUNK_TILES // TILES
+CHUNKS = B // CHUNK_ROWS
+LOAD_TILES = ((8, 8, 16), (16, 16), (32,), (16, 16))
+STORE_TILES = ((32,), (32,), (32,), (16, 16))
 XT_TILES = 2
 Y_TILES = 4
-LOADS_AHEAD = 13
+X_CHUNKS = 3
 
 FLOPS = 2 * B * DIN * DOUT + 2 * DIN * DIN * DOUT
 
@@ -31,32 +36,38 @@ def tile_orthogonaldense_pb_t_kernel(tc, x, u_prev, v_last, d, bias, out):
     nc = tc.nc
     with ExitStack() as ctx:
         consts = ctx.enter_context(tc.tile_pool(name="consts", bufs=1))
-        x_pool = ctx.enter_context(tc.tile_pool(name="x_pool", bufs=LOADS_AHEAD))
-        y_pool = ctx.enter_context(tc.tile_pool(name="y_pool", bufs=ROUNDS))
+        x_pool = ctx.enter_context(tc.tile_pool(name="x_pool", bufs=X_CHUNKS))
+        y_pool = ctx.enter_context(tc.tile_pool(name="y_pool", bufs=CHUNKS))
         work = ctx.enter_context(tc.tile_pool(name="work", bufs=3))
         psum_t = ctx.enter_context(tc.psum_pool(name="psum_t", bufs=6))
         psum_y = ctx.enter_context(tc.psum_pool(name="psum_y", bufs=2))
         ctx.enter_context(tc.manual_schedule())
 
         x_tiles = {}
+        y_tiles = {}
         grouped_tiles = {}
         code_tiles = {}
 
-        def load_x(i):
-            x_sb = x_pool.tile([P, TILES * DIN], BF16, tag="x_sb")
-            rows = x[i * ROUND_ROWS : (i + 1) * ROUND_ROWS, :]
-            nc.sync.dma_start(out=x_sb[:], in_=rows.rearrange("(p r) k -> p (r k)", r=TILES))
-            x_tiles[i] = x_sb
+        def load_x(c):
+            x_sb = x_pool.tile([P, CHUNK_TILES * DIN], BF16, tag="x_sb")
+            rows = x[c * CHUNK_ROWS : (c + 1) * CHUNK_ROWS, :].rearrange("(p r) k -> p (r k)", r=CHUNK_TILES)
+            first = 0
+            for tiles in LOAD_TILES[c]:
+                cols = slice(first * DIN, (first + tiles) * DIN)
+                nc.sync.dma_start(out=x_sb[:, cols], in_=rows[:, cols])
+                first += tiles
+            x_tiles[c] = x_sb
 
         def transpose_round(i):
-            x_words = x_tiles[i][:].bitcast(F32)
+            x_words = x_tiles[i // CHUNK_ROUNDS][:].bitcast(F32)
+            chunk_tile = i % CHUNK_ROUNDS * TILES
             grouped = work.tile([P, TILES * P * PACK], BF16, tag="grouped", align_bytes=64)
             grouped_words = grouped[:].bitcast(F32).rearrange("p (r m u) -> p r m u", r=TILES, u=2)
             for r0 in range(0, TILES, XT_TILES):
                 xt = psum_t.tile([P, XT_TILES, 2, P], F32, tag="t")
                 for a in range(XT_TILES):
                     for u in range(2):
-                        first = (r0 + a) * WORDS + u * P
+                        first = (chunk_tile + r0 + a) * WORDS + u * P
                         nc.tensor.transpose(xt[:, a, u, :], x_words[:, first : first + P], ident_f32[:])
                 nc.scalar.copy(
                     out=grouped_words[:, r0 : r0 + XT_TILES, :, :],
@@ -72,7 +83,12 @@ def tile_orthogonaldense_pb_t_kernel(tc, x, u_prev, v_last, d, bias, out):
 
         def multiply_round(i):
             codes, scales = code_tiles[i]
-            y_sb = y_pool.tile([P, TILES, DOUT], F32, tag="y_sb")
+            c = i // CHUNK_ROUNDS
+            chunk_tile = i % CHUNK_ROUNDS * TILES
+            if chunk_tile == 0:
+                y_sb = y_pool.tile([P, CHUNK_TILES, DOUT], F32, tag="y_sb")
+                y_tiles[c] = y_sb
+            y_sb = y_tiles[c]
             for r0 in range(0, TILES, Y_TILES):
                 y_ps = psum_y.tile([P, Y_TILES, DOUT], F32, tag="y")
                 for a in range(Y_TILES):
@@ -87,16 +103,20 @@ def tile_orthogonaldense_pb_t_kernel(tc, x, u_prev, v_last, d, bias, out):
                         stop=True,
                     )
                 nc.vector.tensor_tensor(
-                    out=y_sb[:, r0 : r0 + Y_TILES, :],
+                    out=y_sb[:, chunk_tile + r0 : chunk_tile + r0 + Y_TILES, :],
                     in0=y_ps[:],
                     in1=bias_all.unsqueeze(1).to_broadcast([P, Y_TILES, DOUT]),
                     op=ADD,
                 )
-            rows = out[i * ROUND_ROWS : (i + 1) * ROUND_ROWS, :]
-            nc.sync.dma_start(
-                out=rows.rearrange("(p r) j -> p (r j)", r=TILES),
-                in_=y_sb[:].rearrange("p r j -> p (r j)"),
-            )
+            rows = out[c * CHUNK_ROWS : (c + 1) * CHUNK_ROWS, :].rearrange("(p r) j -> p (r j)", r=CHUNK_TILES)
+            first = 0
+            for tiles in STORE_TILES[c]:
+                if first + tiles == chunk_tile + TILES:
+                    nc.sync.dma_start(
+                        out=rows[:, first * DOUT : (first + tiles) * DOUT],
+                        in_=y_sb[:, first : first + tiles, :].rearrange("p r j -> p (r j)"),
+                    )
+                first += tiles
 
         ident_bf16 = consts.tile([P, P], BF16)
         make_identity(nc, ident_bf16[:])
@@ -114,8 +134,8 @@ def tile_orthogonaldense_pb_t_kernel(tc, x, u_prev, v_last, d, bias, out):
         nc.sync.dma_start(out=vectors[0:1, 0:DIN], in_=v_last.rearrange("(o n) -> o n", o=1))
         nc.sync.dma_start(out=vectors[0:1, DIN : DIN + DOUT], in_=d.rearrange("(o n) -> o n", o=1))
         nc.sync.dma_start(out=vectors[0:1, DIN + DOUT :], in_=bias.rearrange("(o n) -> o n", o=1))
-        for i in range(LOADS_AHEAD):
-            load_x(i)
+        for c in range(X_CHUNKS):
+            load_x(c)
 
         v_all_ps = psum_t.tile([P, DIN], F32, tag="t")
         nc.tensor.matmul(v_all_ps[:], lhsT=ones[:], rhs=vectors[:, 0:DIN], start=True, stop=True)
@@ -181,7 +201,6 @@ def tile_orthogonaldense_pb_t_kernel(tc, x, u_prev, v_last, d, bias, out):
         )
 
         transpose_round(0)
-        load_x(LOADS_AHEAD)
 
         w_ps = psum_y.tile([P, PACK, DOUT], F32, tag="y")
         for t in range(PACK):
@@ -212,8 +231,8 @@ def tile_orthogonaldense_pb_t_kernel(tc, x, u_prev, v_last, d, bias, out):
         for i in range(ROUNDS + 1):
             if i + 1 < ROUNDS:
                 transpose_round(i + 1)
-            if i + 1 + LOADS_AHEAD < ROUNDS:
-                load_x(i + 1 + LOADS_AHEAD)
+            if (i + 2) % CHUNK_ROUNDS == 0 and (i + 2) // CHUNK_ROUNDS - 1 + X_CHUNKS < CHUNKS:
+                load_x((i + 2) // CHUNK_ROUNDS - 1 + X_CHUNKS)
             if i < ROUNDS:
                 quantise_round(i)
             if i >= 1:

@@ -23,8 +23,8 @@ CHUNK_TILES = 32
 CHUNK_ROWS = P * CHUNK_TILES
 CHUNK_ROUNDS = CHUNK_TILES // TILES
 CHUNKS = B // CHUNK_ROWS
-LOAD_TILES = ((8, 8, 16), (16, 16), (32,), (16, 16))
-STORE_TILES = ((32,), (32,), (32,), (16, 16))
+LOAD_TILES = ((8, 8, 8, 8), (8, 8, 8, 8), (8, 8, 8, 8), (8, 8, 8, 8))
+STORE_TILES = ((32,), (32,), (32,), (16, 8, 8))
 XT_TILES = 2
 Y_TILES = 4
 X_CHUNKS = 3

@@ -23,7 +23,7 @@ CHUNK_TILES = 32
 CHUNK_ROWS = P * CHUNK_TILES
 CHUNK_ROUNDS = CHUNK_TILES // TILES
 CHUNKS = B // CHUNK_ROWS
-LOAD_TILES = ((8, 8, 8, 8), (8, 8, 8, 8), (8, 8, 8, 8), (8, 8, 8, 8))
+LOAD_TILES = ((8, 8, 16), (16, 16), (16, 16), (16, 16))
 STORE_TILES = ((32,), (32,), (32,), (16, 8, 8))
 XT_TILES = 2
 Y_TILES = 4

from contextlib import ExitStack

import concourse.mybir as mybir
from concourse.masks import make_identity

BF16 = mybir.dt.bfloat16
F32 = mybir.dt.float32
U32 = mybir.dt.uint32
U8 = mybir.dt.uint8
FP8X4 = mybir.dt.float8_e4m3fn_x4
ADD = mybir.AluOpType.add
MULT = mybir.AluOpType.mult
SQUARE = mybir.ActivationFunctionType.Square

P = 128
PACK = 4
B, DIN, DOUT = 16384, 512, 128
WORDS = DIN // 2

TILES = 8
ROUNDS = B // (P * TILES)
CHUNK_TILES = 32
CHUNK_ROWS = P * CHUNK_TILES
CHUNK_ROUNDS = CHUNK_TILES // TILES
CHUNKS = B // CHUNK_ROWS
LOAD_TILES = ((8, 8, 16), (16, 16), (16, 16), (16, 16))
STORE_TILES = ((32,), (32,), (32,), (16, 8, 8))
XT_TILES = 2
Y_TILES = 4
X_CHUNKS = 3

FLOPS = 2 * B * DIN * DOUT + 2 * DIN * DIN * DOUT


def tile_orthogonaldense_pb_t_kernel(tc, x, u_prev, v_last, d, bias, out):
    nc = tc.nc
    with ExitStack() as ctx:
        consts = ctx.enter_context(tc.tile_pool(name="consts", bufs=1))
        x_pool = ctx.enter_context(tc.tile_pool(name="x_pool", bufs=X_CHUNKS))
        y_pool = ctx.enter_context(tc.tile_pool(name="y_pool", bufs=CHUNKS))
        work = ctx.enter_context(tc.tile_pool(name="work", bufs=3))
        psum_t = ctx.enter_context(tc.psum_pool(name="psum_t", bufs=6))
        psum_y = ctx.enter_context(tc.psum_pool(name="psum_y", bufs=2))
        ctx.enter_context(tc.manual_schedule())

        x_tiles = {}
        y_tiles = {}
        grouped_tiles = {}
        code_tiles = {}

        def load_x(c):
            x_sb = x_pool.tile([P, CHUNK_TILES * DIN], BF16, tag="x_sb")
            rows = x[c * CHUNK_ROWS : (c + 1) * CHUNK_ROWS, :].rearrange("(p r) k -> p (r k)", r=CHUNK_TILES)
            first = 0
            for tiles in LOAD_TILES[c]:
                cols = slice(first * DIN, (first + tiles) * DIN)
                nc.sync.dma_start(out=x_sb[:, cols], in_=rows[:, cols])
                first += tiles
            x_tiles[c] = x_sb

        def transpose_round(i):
            x_words = x_tiles[i // CHUNK_ROUNDS][:].bitcast(F32)
            chunk_tile = i % CHUNK_ROUNDS * TILES
            grouped = work.tile([P, TILES * P * PACK], BF16, tag="grouped", align_bytes=64)
            grouped_words = grouped[:].bitcast(F32).rearrange("p (r m u) -> p r m u", r=TILES, u=2)
            for r0 in range(0, TILES, XT_TILES):
                xt = psum_t.tile([P, XT_TILES, 2, P], F32, tag="t")
                for a in range(XT_TILES):
                    for u in range(2):
                        first = (chunk_tile + r0 + a) * WORDS + u * P
                        nc.tensor.transpose(xt[:, a, u, :], x_words[:, first : first + P], ident_f32[:])
                nc.scalar.copy(
                    out=grouped_words[:, r0 : r0 + XT_TILES, :, :],
                    in_=xt[:].rearrange("p a u m -> p a m u"),
                )
            grouped_tiles[i] = grouped

        def quantise_round(i):
            codes = work.tile([P, TILES * P], U32, tag="codes", align_bytes=64)
            scales = work.tile([P, TILES * P], U8, tag="scales", align_bytes=64)
            nc.vector.quantize_mx(out=codes[:].bitcast(FP8X4), scales=scales[:], in_=grouped_tiles[i][:])
            code_tiles[i] = (codes, scales)

        def multiply_round(i):
            codes, scales = code_tiles[i]
            c = i // CHUNK_ROUNDS
            chunk_tile = i % CHUNK_ROUNDS * TILES
            if chunk_tile == 0:
                y_sb = y_pool.tile([P, CHUNK_TILES, DOUT], F32, tag="y_sb")
                y_tiles[c] = y_sb
            y_sb = y_tiles[c]
            for r0 in range(0, TILES, Y_TILES):
                y_ps = psum_y.tile([P, Y_TILES, DOUT], F32, tag="y")
                for a in range(Y_TILES):
                    cols = slice((r0 + a) * P, (r0 + a + 1) * P)
                    nc.tensor.matmul_mx(
                        out=y_ps[:, a, :],
                        lhsT=codes[:, cols].bitcast(FP8X4),
                        lhsT_scale=scales[:, cols],
                        rhs=w_codes[:].bitcast(FP8X4),
                        rhs_scale=w_scales[:],
                        start=True,
                        stop=True,
                    )
                nc.vector.tensor_tensor(
                    out=y_sb[:, chunk_tile + r0 : chunk_tile + r0 + Y_TILES, :],
                    in0=y_ps[:],
                    in1=bias_all.unsqueeze(1).to_broadcast([P, Y_TILES, DOUT]),
                    op=ADD,
                )
            rows = out[c * CHUNK_ROWS : (c + 1) * CHUNK_ROWS, :].rearrange("(p r) j -> p (r j)", r=CHUNK_TILES)
            first = 0
            for tiles in STORE_TILES[c]:
                if first + tiles == chunk_tile + TILES:
                    nc.sync.dma_start(
                        out=rows[:, first * DOUT : (first + tiles) * DOUT],
                        in_=y_sb[:, first : first + tiles, :].rearrange("p r j -> p (r j)"),
                    )
                first += tiles

        ident_bf16 = consts.tile([P, P], BF16)
        make_identity(nc, ident_bf16[:])
        ident_f32 = consts.tile([P, P], F32)
        make_identity(nc, ident_f32[:])
        vectors = consts.tile([P, DIN + 2 * DOUT], BF16)
        nc.vector.memset(vectors[:], 0.0)
        ones = consts.tile([P, P], BF16)
        nc.vector.memset(ones[:], 1.0)
        u_sb = consts.tile([P, PACK, DIN], BF16)
        nc.sync.dma_start(
            out=u_sb[:].rearrange("p (u e) k -> p u (e k)", u=2),
            in_=u_prev.rearrange("(u p e) k -> p u (e k)", u=2, e=2),
        )
        nc.sync.dma_start(out=vectors[0:1, 0:DIN], in_=v_last.rearrange("(o n) -> o n", o=1))
        nc.sync.dma_start(out=vectors[0:1, DIN : DIN + DOUT], in_=d.rearrange("(o n) -> o n", o=1))
        nc.sync.dma_start(out=vectors[0:1, DIN + DOUT :], in_=bias.rearrange("(o n) -> o n", o=1))
        for c in range(X_CHUNKS):
            load_x(c)

        v_all_ps = psum_t.tile([P, DIN], F32, tag="t")
        nc.tensor.matmul(v_all_ps[:], lhsT=ones[:], rhs=vectors[:, 0:DIN], start=True, stop=True)
        d_bias_ps = psum_y.tile([P, 2 * DOUT], F32, tag="y")
        nc.tensor.matmul(d_bias_ps[:], lhsT=ones[:], rhs=vectors[:, DIN:], start=True, stop=True)
        vv_ps = psum_t.tile([P, PACK, DOUT], F32, tag="t")
        for s in range(PACK):
            nc.tensor.matmul(
                vv_ps[:, s, :],
                lhsT=vectors[:, s * P : (s + 1) * P],
                rhs=vectors[:, 0:DOUT],
                start=True,
                stop=True,
            )
        v_squares = consts.tile([P, DIN], F32)
        sum_squares = consts.tile([P, 1], F32)
        nc.scalar.activation(out=v_squares[:], in_=v_all_ps[:], func=SQUARE, accum_out=sum_squares[:])
        d_bias = consts.tile([P, 2 * DOUT], F32)
        nc.scalar.copy(out=d_bias[:], in_=d_bias_ps[:])
        d_all = d_bias[:, 0:DOUT]
        bias_all = d_bias[:, DOUT:]
        minus_half_sum = consts.tile([P, 1], F32)
        nc.vector.tensor_scalar_mul(out=minus_half_sum[:], in0=sum_squares[:], scalar1=-0.5)
        minus_two_over_sum = consts.tile([P, 1], F32)
        nc.vector.reciprocal(out=minus_two_over_sum[:], in_=minus_half_sum[:])
        h_grouped = consts.tile([P, DOUT, PACK], BF16, align_bytes=64)
        nc.vector.scalar_tensor_tensor(
            out=h_grouped[:, :, 0],
            in0=vv_ps[:, 0, :],
            scalar=minus_two_over_sum[:, 0:1],
            in1=ident_f32[:],
            op0=MULT,
            op1=ADD,
        )
        nc.vector.tensor_scalar_mul(
            out=h_grouped[:, :, 1:PACK],
            in0=vv_ps[:, 1:PACK, :].rearrange("p s j -> p j s"),
            scalar1=minus_two_over_sum[:, 0:1],
        )

        u_grouped = consts.tile([P, PACK, P, PACK], BF16, align_bytes=64)
        for t0 in range(0, PACK, 2):
            ut = psum_t.tile([P, 2, PACK, P], BF16, tag="t")
            for a in range(2):
                for s in range(PACK):
                    nc.tensor.transpose(ut[:, a, s, :], u_sb[:, t0 + a, s * P : (s + 1) * P], ident_bf16[:])
            copy_out = nc.vector.tensor_copy if t0 == 0 else nc.scalar.copy
            copy_out(out=u_grouped[:, t0 : t0 + 2, :, :], in_=ut[:].rearrange("p a s m -> p a m s"))

        h_codes = consts.tile([P, DOUT], U32, align_bytes=64)
        h_scales = consts.tile([P, DOUT], U8, align_bytes=64)
        nc.vector.quantize_mx(
            out=h_codes[:].bitcast(FP8X4),
            scales=h_scales[:],
            in_=h_grouped[:].rearrange("p j s -> p (j s)"),
        )
        u_codes = consts.tile([P, PACK * P], U32, align_bytes=64)
        u_scales = consts.tile([P, PACK * P], U8, align_bytes=64)
        nc.vector.quantize_mx(
            out=u_codes[:].bitcast(FP8X4),
            scales=u_scales[:],
            in_=u_grouped[:].rearrange("p t m s -> p (t m s)"),
        )

        transpose_round(0)

        w_ps = psum_y.tile([P, PACK, DOUT], F32, tag="y")
        for t in range(PACK):
            nc.tensor.matmul_mx(
                out=w_ps[:, t, :],
                lhsT=u_codes[:, t * P : (t + 1) * P].bitcast(FP8X4),
                lhsT_scale=u_scales[:, t * P : (t + 1) * P],
                rhs=h_codes[:].bitcast(FP8X4),
                rhs_scale=h_scales[:],
                start=True,
                stop=True,
            )
        w_grouped = consts.tile([P, DOUT, PACK], BF16, align_bytes=64)
        nc.vector.tensor_tensor(
            out=w_grouped[:],
            in0=w_ps[:].rearrange("p t j -> p j t"),
            in1=d_all.unsqueeze(2).to_broadcast([P, DOUT, PACK]),
            op=MULT,
        )
        w_codes = consts.tile([P, DOUT], U32, align_bytes=64)
        w_scales = consts.tile([P, DOUT], U8, align_bytes=64)
        nc.vector.quantize_mx(
            out=w_codes[:].bitcast(FP8X4),
            scales=w_scales[:],
            in_=w_grouped[:].rearrange("p j t -> p (j t)"),
        )

        for i in range(ROUNDS + 1):
            if i + 1 < ROUNDS:
                transpose_round(i + 1)
            if (i + 2) % CHUNK_ROUNDS == 0 and (i + 2) // CHUNK_ROUNDS - 1 + X_CHUNKS < CHUNKS:
                load_x((i + 2) // CHUNK_ROUNDS - 1 + X_CHUNKS)
            if i < ROUNDS:
                quantise_round(i)
            if i >= 1:
                multiply_round(i - 1)
